import numpy as np
import ml_dtypes


def mxq(x, axis, fmt="e4m3"):
    dtype, down = {"e4m3": (ml_dtypes.float8_e4m3fn, 7), "e5m2": (ml_dtypes.float8_e5m2, 14)}[fmt]
    v = np.moveaxis(np.asarray(x, np.float32).astype(ml_dtypes.bfloat16).astype(np.float64), axis, -1)
    blocks = v.reshape(v.shape[:-1] + (-1, 32))
    amax = np.abs(blocks).max(-1, keepdims=True)
    byte = np.maximum(np.where(amax > 0, np.frexp(amax)[1] - 1 + 127, 0) - down, 1)
    scale = np.exp2(byte - 127.0)
    codes = (blocks / scale).astype(np.float32).astype(dtype).astype(np.float64)
    return np.moveaxis((codes * scale).reshape(v.shape), -1, axis)


WIDE = False


def mx_kscale(k):
    if not WIDE:
        return np.ones(k)
    levels = np.array([10, -10, 5, -5, 0])
    if k % 512:
        return np.exp2(np.random.permutation(np.resize(levels, k // 32))).repeat(32)
    a = np.empty((k // 512, 16))
    for p in range(k // 512):
        a[p, :8] = np.random.permutation(np.resize(levels, 8))
        for g in range(8):
            far = levels[np.abs(levels - a[p, g]) >= 10]
            a[p, g + 8] = far[np.random.randint(len(far))]
    return np.exp2(a.ravel()).repeat(32)


BF16 = ml_dtypes.bfloat16


def bf(x):
    return np.asarray(x, np.float32).astype(BF16)


def f64(x):
    return np.asarray(x).astype(np.float64)


S, D, N_HEADS, N_KV_HEADS, HEAD_DIM = 512, 2048, 16, 4, 128
Q_DIM = N_HEADS * HEAD_DIM
KV_DIM = N_KV_HEADS * HEAD_DIM
ROPE_THETA = 500000.0


def apply_rope(t, cos, sin):
    te = t[:, :, ::2]
    to = t[:, :, 1::2]
    c = cos[:, None, :]
    s = sin[:, None, :]
    te_rot = te * c - to * s
    to_rot = te * s + to * c
    return np.stack([te_rot, to_rot], axis=-1).reshape(t.shape)


def setup_inputs():
    s = mx_kscale(D)
    inv_freq = 1.0 / ROPE_THETA ** (np.arange(0, HEAD_DIM, 2) / HEAD_DIM)
    angles = np.arange(S)[:, None] * inv_freq[None, :]
    return {"x": bf(np.random.standard_normal((S, D)) * s),
            "freqs_cos": bf(np.cos(angles)),
            "freqs_sin": bf(np.sin(angles)),
            "wqkv": bf(np.random.standard_normal((Q_DIM + 2 * KV_DIM, D)) / np.sqrt(D) / s[None, :])}


def reference(x, freqs_cos, freqs_sin, wqkv):
    qkv = mxq(f64(x), 1, "e4m3") @ mxq(f64(wqkv), 1, "e4m3").T
    q = qkv[:, :Q_DIM].reshape(S, N_HEADS, HEAD_DIM)
    k = qkv[:, Q_DIM:Q_DIM + KV_DIM].reshape(S, N_KV_HEADS, HEAD_DIM)
    v = qkv[:, Q_DIM + KV_DIM:].reshape(S, N_KV_HEADS, HEAD_DIM)
    cos, sin = f64(freqs_cos), f64(freqs_sin)
    return apply_rope(q, cos, sin), apply_rope(k, cos, sin), v

@@ -1,0 +1,188 @@
+from contextlib import ExitStack
+
+import concourse.mybir as mybir
+from concourse.masks import make_identity
+
+F32 = mybir.dt.float32
+BF16 = mybir.dt.bfloat16
+U32 = mybir.dt.uint32
+U8 = mybir.dt.uint8
+FP8X4 = mybir.dt.float8_e4m3fn_x4
+MULT = mybir.AluOpType.mult
+ADD = mybir.AluOpType.add
+
+P = 128
+S = 512
+D = 2048
+Q_DIM = 2048
+KV_DIM = 512
+HEAD_DIM = 128
+PAIRS = HEAD_DIM // 2
+
+PACK = 4
+K_PASS = P * PACK
+PASSES = D // K_PASS
+WORD_HALVES = 2
+UNIT = 256
+UNIT_TILES = UNIT // P
+X_UNITS = S // UNIT
+W_UNITS = (Q_DIM + 2 * KV_DIM) // UNIT
+ROTATED_UNITS = (Q_DIM + KV_DIM) // UNIT
+UNIT_HEADS = UNIT // HEAD_DIM
+TOKEN_TILES = S // P
+STORE_UNITS = 2
+STORE_COLS = STORE_UNITS * UNIT
+LOADS_AHEAD = 6
+
+FLOPS = 2 * S * (Q_DIM + 2 * KV_DIM) * D
+
+assert KV_DIM == STORE_COLS
+
+
+def tile_mha_pa_kernel(tc, x, freqs_cos, freqs_sin, wqkv, out_0, out_1, out_2):
+    nc = tc.nc
+
+    x_units = x.rearrange("(p n j) k -> n p j k", n=X_UNITS, j=UNIT_TILES)
+    cos_rows = freqs_cos.rearrange("(p m) i -> p m i", m=TOKEN_TILES)
+    sin_rows = freqs_sin.rearrange("(p m) i -> p m i", m=TOKEN_TILES)
+    w_units = wqkv.rearrange("(n p j) k -> n p j k", p=P, j=UNIT_TILES)
+    q_rows = out_0.rearrange("(p m) h d -> p m (h d)", m=TOKEN_TILES)
+    k_rows = out_1.rearrange("(p m) h d -> p m (h d)", m=TOKEN_TILES)
+    v_rows = out_2.rearrange("(p m) h d -> p m (h d)", m=TOKEN_TILES)
+    store_targets = [q_rows[:, :, c : c + STORE_COLS] for c in range(0, Q_DIM, STORE_COLS)] + [k_rows, v_rows]
+
+    with ExitStack() as ctx:
+        const = ctx.enter_context(tc.tile_pool(name="const", bufs=1))
+        raw_pool = ctx.enter_context(tc.tile_pool(name="raw", bufs=1))
+        grouped_pool = ctx.enter_context(tc.tile_pool(name="grouped", bufs=3))
+        w_mx_pool = ctx.enter_context(tc.tile_pool(name="w_mx", bufs=3))
+        product_pool = ctx.enter_context(tc.tile_pool(name="product", bufs=4))
+        result_pool = ctx.enter_context(tc.tile_pool(name="result", bufs=3))
+        flipped_pool = ctx.enter_context(tc.psum_pool(name="flipped", bufs=PASSES))
+        acc_pool = ctx.enter_context(tc.psum_pool(name="acc", bufs=2 * X_UNITS))
+        ctx.enter_context(tc.manual_schedule())
+
+        def load_unit(rows, name):
+            raw = raw_pool.tile([P, UNIT_TILES, D], BF16, name=name)
+            nc.sync.dma_start(out=raw[:], in_=rows)
+            return raw
+
+        cos_sb = const.tile([P, TOKEN_TILES, PAIRS], BF16)
+        sin_sb = const.tile([P, TOKEN_TILES, PAIRS], BF16)
+        nc.scalar.dma_start(out=cos_sb[:], in_=cos_rows)
+        nc.scalar.dma_start(out=sin_sb[:], in_=sin_rows)
+        x_raw = [load_unit(x_units[n, :, :, :], "x_raw%d" % n) for n in range(X_UNITS)]
+        w_raw = [load_unit(w_units[n, :, :, :], "w_raw%d" % n) for n in range(LOADS_AHEAD)]
+
+        ident = const.tile([P, P], F32)
+        make_identity(nc, ident[:])
+
+        first_table = const.tile([P, TOKEN_TILES, UNIT_HEADS, PAIRS, 2], F32)
+        second_table = const.tile([P, TOKEN_TILES, UNIT_HEADS, PAIRS, 2], F32)
+        over_heads = [P, TOKEN_TILES, UNIT_HEADS, PAIRS]
+        cos_heads = cos_sb[:].unsqueeze(2).to_broadcast(over_heads)
+        sin_heads = sin_sb[:].unsqueeze(2).to_broadcast(over_heads)
+        nc.vector.tensor_copy(out=first_table[:, :, :, :, 0], in_=cos_heads)
+        nc.vector.tensor_copy(out=first_table[:, :, :, :, 1], in_=sin_heads)
+        nc.vector.tensor_scalar_mul(out=second_table[:, :, :, :, 0], in0=sin_heads, scalar1=-1.0)
+        nc.vector.tensor_copy(out=second_table[:, :, :, :, 1], in_=cos_heads)
+
+        def transpose_unit(raw):
+            grouped = grouped_pool.tile([P, PASSES * UNIT * PACK], BF16, align_bytes=64)
+            grouped_words = grouped[:].bitcast(F32).rearrange(
+                "p (g j r u) -> p g j r u", g=PASSES, j=UNIT_TILES, u=WORD_HALVES
+            )
+            for g in range(PASSES):
+                flipped = flipped_pool.tile([P, UNIT_TILES, WORD_HALVES, P], F32)
+                for j in range(UNIT_TILES):
+                    raw_words = raw[:, j, :].bitcast(F32)
+                    for u in range(WORD_HALVES):
+                        words = slice(WORD_HALVES * P * g + u, WORD_HALVES * P * (g + 1), WORD_HALVES)
+                        nc.tensor.transpose(flipped[:, j, u, :], raw_words[:, words], ident[:])
+                nc.scalar.copy(out=grouped_words[:, g, :, :, :], in_=flipped[:].rearrange("p j u r -> p j r u"))
+            return grouped
+
+        def quantise_unit(grouped, pool, name):
+            codes = pool.tile([P, PASSES, UNIT], U32, name=name + "_codes", align_bytes=64)
+            scales = pool.tile([P, PASSES, UNIT], U8, name=name + "_scales", align_bytes=64)
+            nc.vector.quantize_mx(
+                out=codes[:].rearrange("p g c -> p (g c)").bitcast(FP8X4),
+                scales=scales[:].rearrange("p g c -> p (g c)"),
+                in_=grouped[:],
+            )
+            return codes, scales
+
+        def multiply(x_unit, w_unit):
+            x_codes, x_scales = x_unit
+            w_codes, w_scales = w_unit
+            acc = acc_pool.tile([P, UNIT_TILES, UNIT], F32)
+            for j in range(UNIT_TILES):
+                tokens = slice(j * P, (j + 1) * P)
+                for g in range(PASSES):
+                    nc.tensor.matmul_mx(
+                        out=acc[:, j, :],
+                        lhsT=x_codes[:, g, tokens].bitcast(FP8X4),
+                        lhsT_scale=x_scales[:, g, tokens],
+                        rhs=w_codes[:, g, :].bitcast(FP8X4),
+                        rhs_scale=w_scales[:, g, :],
+                        start=(g == 0),
+                        stop=(g == PASSES - 1),
+                    )
+            return acc
+
+        def rotate(acc, tiles, rotated):
+            pair_shape = [P, UNIT_TILES, P, 2]
+            from_first = product_pool.tile(pair_shape, F32)
+            from_second = product_pool.tile(pair_shape, F32)
+            nc.vector.tensor_tensor(
+                out=from_first[:],
+                in0=acc[:, :, 0:P].unsqueeze(3).to_broadcast(pair_shape),
+                in1=first_table[:, tiles, :, :, :].rearrange("p m h i e -> p m (h i) e"),
+                op=MULT,
+            )
+            nc.vector.tensor_tensor(
+                out=from_second[:],
+                in0=acc[:, :, P:UNIT].unsqueeze(3).to_broadcast(pair_shape),
+                in1=second_table[:, tiles, :, :, :].rearrange("p m h i e -> p m (h i) e"),
+                op=MULT,
+            )
+            nc.gpsimd.tensor_tensor(
+                out=rotated,
+                in0=from_first[:].rearrange("p m r e -> p m (r e)"),
+                in1=from_second[:].rearrange("p m r e -> p m (r e)"),
+                op=ADD,
+            )
+
+        def interleave(acc, plain):
+            nc.scalar.copy(
+                out=plain.rearrange("p m (r j) -> p m r j", j=UNIT_TILES),
+                in_=acc[:].rearrange("p m (j r) -> p m r j", j=UNIT_TILES),
+            )
+
+        x_grouped = [transpose_unit(x_raw[n]) for n in range(X_UNITS)]
+        x_mx = [quantise_unit(x_grouped[n], const, "x%d" % n) for n in range(X_UNITS)]
+        w_mx = quantise_unit(transpose_unit(w_raw[0]), w_mx_pool, "w")
+
+        result = None
+        for n in range(W_UNITS):
+            if n + LOADS_AHEAD < W_UNITS:
+                w_raw.append(load_unit(w_units[n + LOADS_AHEAD, :, :, :], "w_raw%d" % (n + LOADS_AHEAD)))
+            following = n + 1 < W_UNITS
+            if following:
+                w_grouped = transpose_unit(w_raw[n + 1])
+            banks = [multiply(x_mx[b], w_mx) for b in range(X_UNITS)]
+            if following:
+                w_mx = quantise_unit(w_grouped, w_mx_pool, "w")
+
+            part = n % STORE_UNITS
+            if part == 0:
+                result = result_pool.tile([P, TOKEN_TILES, STORE_COLS], F32, name="result")
+            for b in range(X_UNITS):
+                tiles = slice(b * UNIT_TILES, (b + 1) * UNIT_TILES)
+                unit_result = result[:, tiles, part * UNIT : (part + 1) * UNIT]
+                if n < ROTATED_UNITS:
+                    rotate(banks[b], tiles, unit_result)
+                else:
+                    interleave(banks[b], unit_result)
+                if part == STORE_UNITS - 1:
+                    nc.sync.dma_start(out=store_targets[n // STORE_UNITS][:, tiles, :], in_=result[:, tiles, :])

@@ -23,16 +23,19 @@ PACK = 4
 K_PASS = P * PACK
 PASSES = D // K_PASS
 WORD_HALVES = 2
+WORDS = D // 2
+BANK_PASSES = 2
 UNIT = 256
 UNIT_TILES = UNIT // P
-X_UNITS = S // UNIT
 W_UNITS = (Q_DIM + 2 * KV_DIM) // UNIT
 ROTATED_UNITS = (Q_DIM + KV_DIM) // UNIT
 UNIT_HEADS = UNIT // HEAD_DIM
 TOKEN_TILES = S // P
+BANKS = TOKEN_TILES // 2
 STORE_UNITS = 2
 STORE_COLS = STORE_UNITS * UNIT
 LOADS_AHEAD = 6
+STRIDED_UNITS = 2
 
 FLOPS = 2 * S * (Q_DIM + 2 * KV_DIM) * D
 
@@ -42,7 +45,7 @@ assert KV_DIM == STORE_COLS
 def tile_mha_pa_kernel(tc, x, freqs_cos, freqs_sin, wqkv, out_0, out_1, out_2):
     nc = tc.nc
 
-    x_units = x.rearrange("(p n j) k -> n p j k", n=X_UNITS, j=UNIT_TILES)
+    x_rows = x.rearrange("(p m) k -> m p k", m=TOKEN_TILES)
     cos_rows = freqs_cos.rearrange("(p m) i -> p m i", m=TOKEN_TILES)
     sin_rows = freqs_sin.rearrange("(p m) i -> p m i", m=TOKEN_TILES)
     w_units = wqkv.rearrange("(n p j) k -> n p j k", p=P, j=UNIT_TILES)
@@ -54,57 +57,85 @@ def tile_mha_pa_kernel(tc, x, freqs_cos, freqs_sin, wqkv, out_0, out_1, out_2):
     with ExitStack() as ctx:
         const = ctx.enter_context(tc.tile_pool(name="const", bufs=1))
         raw_pool = ctx.enter_context(tc.tile_pool(name="raw", bufs=1))
+        ordered_pool = ctx.enter_context(tc.tile_pool(name="ordered", bufs=4))
         grouped_pool = ctx.enter_context(tc.tile_pool(name="grouped", bufs=3))
         w_mx_pool = ctx.enter_context(tc.tile_pool(name="w_mx", bufs=3))
         product_pool = ctx.enter_context(tc.tile_pool(name="product", bufs=4))
         result_pool = ctx.enter_context(tc.tile_pool(name="result", bufs=3))
-        flipped_pool = ctx.enter_context(tc.psum_pool(name="flipped", bufs=PASSES))
-        acc_pool = ctx.enter_context(tc.psum_pool(name="acc", bufs=2 * X_UNITS))
+        flipped_pool = ctx.enter_context(tc.psum_pool(name="flipped", bufs=4))
+        acc_pool = ctx.enter_context(tc.psum_pool(name="acc", bufs=2 * BANKS))
         ctx.enter_context(tc.manual_schedule())
-
-        def load_unit(rows, name):
-            raw = raw_pool.tile([P, UNIT_TILES, D], BF16, name=name)
-            nc.sync.dma_start(out=raw[:], in_=rows)
-            return raw
 
         cos_sb = const.tile([P, TOKEN_TILES, PAIRS], BF16)
         sin_sb = const.tile([P, TOKEN_TILES, PAIRS], BF16)
         nc.scalar.dma_start(out=cos_sb[:], in_=cos_rows)
         nc.scalar.dma_start(out=sin_sb[:], in_=sin_rows)
-        x_raw = [load_unit(x_units[n, :, :, :], "x_raw%d" % n) for n in range(X_UNITS)]
-        w_raw = [load_unit(w_units[n, :, :, :], "w_raw%d" % n) for n in range(LOADS_AHEAD)]
+        x_raw = []
+        for m in range(TOKEN_TILES):
+            raw = raw_pool.tile([P, D], BF16, name="x_raw%d" % m)
+            nc.sync.dma_start(out=raw[:], in_=x_rows[m, :, :])
+            x_raw.append(raw)
+
+        def load_unit(n):
+            raw = raw_pool.tile([P, UNIT_TILES, D], BF16, name="w_raw%d" % n)
+            if n < STRIDED_UNITS:
+                for j in range(UNIT_TILES):
+                    nc.sync.dma_start(out=raw[:, j, :], in_=w_units[n, :, j, :])
+            else:
+                nc.sync.dma_start(out=raw[:], in_=w_units[n, :, :, :])
+            return raw
+
+        w_raw = [load_unit(n) for n in range(LOADS_AHEAD)]
 
         ident = const.tile([P, P], F32)
         make_identity(nc, ident[:])
 
-        first_table = const.tile([P, TOKEN_TILES, UNIT_HEADS, PAIRS, 2], F32)
-        second_table = const.tile([P, TOKEN_TILES, UNIT_HEADS, PAIRS, 2], F32)
-        over_heads = [P, TOKEN_TILES, UNIT_HEADS, PAIRS]
-        cos_heads = cos_sb[:].unsqueeze(2).to_broadcast(over_heads)
-        sin_heads = sin_sb[:].unsqueeze(2).to_broadcast(over_heads)
-        nc.vector.tensor_copy(out=first_table[:, :, :, :, 0], in_=cos_heads)
-        nc.vector.tensor_copy(out=first_table[:, :, :, :, 1], in_=sin_heads)
-        nc.vector.tensor_scalar_mul(out=second_table[:, :, :, :, 0], in0=sin_heads, scalar1=-1.0)
-        nc.vector.tensor_copy(out=second_table[:, :, :, :, 1], in_=cos_heads)
+        planes = const.tile([P, TOKEN_TILES, 3, UNIT_HEADS, PAIRS], BF16)
 
-        def transpose_unit(raw):
-            grouped = grouped_pool.tile([P, PASSES * UNIT * PACK], BF16, align_bytes=64)
-            grouped_words = grouped[:].bitcast(F32).rearrange(
+        def make_planes():
+            over_heads = [P, TOKEN_TILES, UNIT_HEADS, PAIRS]
+            cos_heads = cos_sb[:].unsqueeze(2).to_broadcast(over_heads)
+            sin_heads = sin_sb[:].unsqueeze(2).to_broadcast(over_heads)
+            nc.vector.tensor_scalar_mul(out=planes[:, :, 0, :, :], in0=sin_heads, scalar1=-1.0)
+            nc.vector.tensor_copy(out=planes[:, :, 1, :, :], in_=cos_heads)
+            nc.vector.tensor_copy(out=planes[:, :, 2, :, :], in_=sin_heads)
+
+        def put_in_order(copy, raw):
+            ordered = ordered_pool.tile([P, D], BF16, name="ordered")
+            copy(
+                out=ordered[:].bitcast(F32).rearrange("p (g u m) -> p g u m", g=PASSES, u=WORD_HALVES),
+                in_=raw.bitcast(F32).rearrange("p (g m u) -> p g u m", g=PASSES, u=WORD_HALVES),
+            )
+            return ordered
+
+        def transpose_tile(raw, ordered, target, copies):
+            words = raw.bitcast(F32) if ordered is None else ordered[:].bitcast(F32)
+            for first, copy in zip(range(0, PASSES, BANK_PASSES), copies):
+                flipped = flipped_pool.tile([P, BANK_PASSES, WORD_HALVES, P], F32, name="flipped")
+                for b in range(BANK_PASSES):
+                    for u in range(WORD_HALVES):
+                        start = (first + b) * WORD_HALVES * P
+                        if ordered is None:
+                            cols = words[:, start + u : start + WORD_HALVES * P : WORD_HALVES]
+                        else:
+                            cols = words[:, start + u * P : start + (u + 1) * P]
+                        nc.tensor.transpose(flipped[:, b, u, :], cols, ident[:])
+                copy(
+                    out=target[:, first : first + BANK_PASSES, :, :], in_=flipped[:].rearrange("p b u r -> p b r u")
+                )
+
+        def transpose_unit(raw, ordered, copies):
+            grouped = grouped_pool.tile([P, PASSES * UNIT * PACK], BF16, name="grouped", align_bytes=64)
+            words = grouped[:].bitcast(F32).rearrange(
                 "p (g j r u) -> p g j r u", g=PASSES, j=UNIT_TILES, u=WORD_HALVES
             )
-            for g in range(PASSES):
-                flipped = flipped_pool.tile([P, UNIT_TILES, WORD_HALVES, P], F32)
-                for j in range(UNIT_TILES):
-                    raw_words = raw[:, j, :].bitcast(F32)
-                    for u in range(WORD_HALVES):
-                        words = slice(WORD_HALVES * P * g + u, WORD_HALVES * P * (g + 1), WORD_HALVES)
-                        nc.tensor.transpose(flipped[:, j, u, :], raw_words[:, words], ident[:])
-                nc.scalar.copy(out=grouped_words[:, g, :, :, :], in_=flipped[:].rearrange("p j u r -> p j r u"))
+            for j in range(UNIT_TILES):
+                transpose_tile(raw[:, j, :], ordered[j], words[:, :, j, :, :], copies)
             return grouped
 
-        def quantise_unit(grouped, pool, name):
-            codes = pool.tile([P, PASSES, UNIT], U32, name=name + "_codes", align_bytes=64)
-            scales = pool.tile([P, PASSES, UNIT], U8, name=name + "_scales", align_bytes=64)
+        def quantise(grouped, rows, pool, name):
+            codes = pool.tile([P, PASSES, rows], U32, name=name + "_codes", align_bytes=64)
+            scales = pool.tile([P, PASSES, rows], U8, name=name + "_scales", align_bytes=64)
             nc.vector.quantize_mx(
                 out=codes[:].rearrange("p g c -> p (g c)").bitcast(FP8X4),
                 scales=scales[:].rearrange("p g c -> p (g c)"),
@@ -112,17 +143,16 @@ def tile_mha_pa_kernel(tc, x, freqs_cos, freqs_sin, wqkv, out_0, out_1, out_2):
             )
             return codes, scales
 
-        def multiply(x_unit, w_unit):
-            x_codes, x_scales = x_unit
+        def multiply(b, w_unit):
             w_codes, w_scales = w_unit
-            acc = acc_pool.tile([P, UNIT_TILES, UNIT], F32)
-            for j in range(UNIT_TILES):
-                tokens = slice(j * P, (j + 1) * P)
+            acc = acc_pool.tile([P, 2, UNIT], F32, name="acc")
+            for j in range(2):
+                x_codes, x_scales = x_mx[2 * b + j]
                 for g in range(PASSES):
                     nc.tensor.matmul_mx(
                         out=acc[:, j, :],
-                        lhsT=x_codes[:, g, tokens].bitcast(FP8X4),
-                        lhsT_scale=x_scales[:, g, tokens],
+                        lhsT=x_codes[:, g, :].bitcast(FP8X4),
+                        lhsT_scale=x_scales[:, g, :],
                         rhs=w_codes[:, g, :].bitcast(FP8X4),
                         rhs_scale=w_scales[:, g, :],
                         start=(g == 0),
@@ -130,22 +160,26 @@ def tile_mha_pa_kernel(tc, x, freqs_cos, freqs_sin, wqkv, out_0, out_1, out_2):
                     )
             return acc
 
-        def rotate(acc, tiles, rotated):
-            pair_shape = [P, UNIT_TILES, P, 2]
-            from_first = product_pool.tile(pair_shape, F32)
-            from_second = product_pool.tile(pair_shape, F32)
+        def products(acc, tiles):
+            pair_shape = [P, 2, P, 2]
+            from_first = product_pool.tile(pair_shape, F32, name="from_first")
+            from_second = product_pool.tile(pair_shape, F32, name="from_second")
             nc.vector.tensor_tensor(
                 out=from_first[:],
                 in0=acc[:, :, 0:P].unsqueeze(3).to_broadcast(pair_shape),
-                in1=first_table[:, tiles, :, :, :].rearrange("p m h i e -> p m (h i) e"),
+                in1=planes[:, tiles, 1:3, :, :].rearrange("p m e h i -> p m (h i) e"),
                 op=MULT,
             )
             nc.vector.tensor_tensor(
                 out=from_second[:],
                 in0=acc[:, :, P:UNIT].unsqueeze(3).to_broadcast(pair_shape),
-                in1=second_table[:, tiles, :, :, :].rearrange("p m h i e -> p m (h i) e"),
+                in1=planes[:, tiles, 0:2, :, :].rearrange("p m e h i -> p m (h i) e"),
                 op=MULT,
             )
+            return from_first, from_second
+
+        def add_products(pair, rotated):
+            from_first, from_second = pair
             nc.gpsimd.tensor_tensor(
                 out=rotated,
                 in0=from_first[:].rearrange("p m r e -> p m (r e)"),
@@ -153,36 +187,84 @@ def tile_mha_pa_kernel(tc, x, freqs_cos, freqs_sin, wqkv, out_0, out_1, out_2):
                 op=ADD,
             )
 
-        def interleave(acc, plain):
-            nc.scalar.copy(
+        def hold_gpsimd(scales):
+            nc.gpsimd.tensor_copy(out=gate[:], in_=scales[:, 0, 0:4])
+
+        def interleave(copy, acc, plain):
+            copy(
                 out=plain.rearrange("p m (r j) -> p m r j", j=UNIT_TILES),
                 in_=acc[:].rearrange("p m (j r) -> p m r j", j=UNIT_TILES),
             )
 
-        x_grouped = [transpose_unit(x_raw[n]) for n in range(X_UNITS)]
-        x_mx = [quantise_unit(x_grouped[n], const, "x%d" % n) for n in range(X_UNITS)]
-        w_mx = quantise_unit(transpose_unit(w_raw[0]), w_mx_pool, "w")
+        def put_unit_in_order(n):
+            raw = w_raw[n]
+            if n < STRIDED_UNITS:
+                return [None, None]
+            return [put_in_order(nc.scalar.copy, raw[:, 0, :]), put_in_order(nc.vector.tensor_copy, raw[:, 1, :])]
+
+        gate = const.tile([P, 4], U8)
+        make_planes()
+
+        x_grouped = []
+        x_mx = []
+        both = [nc.scalar.copy, nc.vector.tensor_copy]
+        alone = [nc.scalar.copy, nc.scalar.copy]
+        for m in range(TOKEN_TILES):
+            if m > 0:
+                x_mx.append(quantise(x_grouped[m - 1], P, const, "x%d" % (m - 1)))
+            grouped = const.tile([P, PASSES * P * PACK], BF16, name="x_grouped%d" % m, align_bytes=64)
+            transpose_tile(
+                x_raw[m][:],
+                None,
+                grouped[:].bitcast(F32).rearrange("p (g r u) -> p g r u", g=PASSES, u=WORD_HALVES),
+                [alone, both][m % 2],
+            )
+            x_grouped.append(grouped)
+        x_mx.append(quantise(x_grouped[-1], P, const, "x_last"))
+        w_grouped = transpose_unit(w_raw[0], [None, None], both)
+        w_mx = quantise(w_grouped, UNIT, w_mx_pool, "w")
+        ordered = [None, None]
 
         result = None
+        late = None
         for n in range(W_UNITS):
             if n + LOADS_AHEAD < W_UNITS:
-                w_raw.append(load_unit(w_units[n + LOADS_AHEAD, :, :, :], "w_raw%d" % (n + LOADS_AHEAD)))
+                w_raw.append(load_unit(n + LOADS_AHEAD))
             following = n + 1 < W_UNITS
             if following:
-                w_grouped = transpose_unit(w_raw[n + 1])
-            banks = [multiply(x_mx[b], w_mx) for b in range(X_UNITS)]
+                w_grouped = transpose_unit(w_raw[n + 1], ordered, alone)
+            if n + 2 < W_UNITS:
+                ordered = put_unit_in_order(n + 2)
+            banks = [multiply(b, w_mx) for b in range(BANKS)]
             if following:
-                w_mx = quantise_unit(w_grouped, w_mx_pool, "w")
+                w_mx = quantise(w_grouped, UNIT, w_mx_pool, "w")
+                if late is not None:
+                    hold_gpsimd(w_mx[1])
+            if late is not None:
+                late()
+                late = None
 
             part = n % STORE_UNITS
             if part == 0:
                 result = result_pool.tile([P, TOKEN_TILES, STORE_COLS], F32, name="result")
-            for b in range(X_UNITS):
-                tiles = slice(b * UNIT_TILES, (b + 1) * UNIT_TILES)
-                unit_result = result[:, tiles, part * UNIT : (part + 1) * UNIT]
-                if n < ROTATED_UNITS:
-                    rotate(banks[b], tiles, unit_result)
-                else:
-                    interleave(banks[b], unit_result)
+
+            def finish(b, pair, n=n, result=result):
+                tiles = slice(2 * b, 2 * b + 2)
+                part = n % STORE_UNITS
+                if pair is not None:
+                    add_products(pair, result[:, tiles, part * UNIT : (part + 1) * UNIT])
                 if part == STORE_UNITS - 1:
                     nc.sync.dma_start(out=store_targets[n // STORE_UNITS][:, tiles, :], in_=result[:, tiles, :])
+
+            if n < ROTATED_UNITS:
+                finish(0, products(banks[0], slice(0, 2)))
+                pair = products(banks[1], slice(2, 4))
+                late = lambda finish=finish, pair=pair: finish(1, pair)
+            else:
+                for b in range(BANKS):
+                    interleave(
+                        [nc.scalar.copy, nc.vector.tensor_copy][b],
+                        banks[b],
+                        result[:, 2 * b : 2 * b + 2, part * UNIT : (part + 1) * UNIT],
+                    )
+                    finish(b, None)

@@ -58,6 +58,7 @@ def tile_mha_pa_kernel(tc, x, freqs_cos, freqs_sin, wqkv, out_0, out_1, out_2):
         const = ctx.enter_context(tc.tile_pool(name="const", bufs=1))
         raw_pool = ctx.enter_context(tc.tile_pool(name="raw", bufs=1))
         ordered_pool = ctx.enter_context(tc.tile_pool(name="ordered", bufs=4))
+        x_grouped_pool = ctx.enter_context(tc.tile_pool(name="x_grouped", bufs=2))
         grouped_pool = ctx.enter_context(tc.tile_pool(name="grouped", bufs=3))
         w_mx_pool = ctx.enter_context(tc.tile_pool(name="w_mx", bufs=3))
         product_pool = ctx.enter_context(tc.tile_pool(name="product", bufs=4))
@@ -90,15 +91,17 @@ def tile_mha_pa_kernel(tc, x, freqs_cos, freqs_sin, wqkv, out_0, out_1, out_2):
         ident = const.tile([P, P], F32)
         make_identity(nc, ident[:])
 
-        planes = const.tile([P, TOKEN_TILES, 3, UNIT_HEADS, PAIRS], BF16)
+        first_table = const.tile([P, TOKEN_TILES, UNIT_HEADS, PAIRS, 2], F32)
+        second_table = const.tile([P, TOKEN_TILES, UNIT_HEADS, PAIRS, 2], F32)
 
-        def make_planes():
+        def make_tables():
             over_heads = [P, TOKEN_TILES, UNIT_HEADS, PAIRS]
             cos_heads = cos_sb[:].unsqueeze(2).to_broadcast(over_heads)
             sin_heads = sin_sb[:].unsqueeze(2).to_broadcast(over_heads)
-            nc.vector.tensor_scalar_mul(out=planes[:, :, 0, :, :], in0=sin_heads, scalar1=-1.0)
-            nc.vector.tensor_copy(out=planes[:, :, 1, :, :], in_=cos_heads)
-            nc.vector.tensor_copy(out=planes[:, :, 2, :, :], in_=sin_heads)
+            nc.vector.tensor_copy(out=first_table[:, :, :, :, 0], in_=cos_heads)
+            nc.vector.tensor_copy(out=first_table[:, :, :, :, 1], in_=sin_heads)
+            nc.vector.tensor_scalar_mul(out=second_table[:, :, :, :, 0], in0=sin_heads, scalar1=-1.0)
+            nc.vector.tensor_copy(out=second_table[:, :, :, :, 1], in_=cos_heads)
 
         def put_in_order(copy, raw):
             ordered = ordered_pool.tile([P, D], BF16, name="ordered")
@@ -167,13 +170,13 @@ def tile_mha_pa_kernel(tc, x, freqs_cos, freqs_sin, wqkv, out_0, out_1, out_2):
             nc.vector.tensor_tensor(
                 out=from_first[:],
                 in0=acc[:, :, 0:P].unsqueeze(3).to_broadcast(pair_shape),
-                in1=planes[:, tiles, 1:3, :, :].rearrange("p m e h i -> p m (h i) e"),
+                in1=first_table[:, tiles, :, :, :].rearrange("p m h i e -> p m (h i) e"),
                 op=MULT,
             )
             nc.vector.tensor_tensor(
                 out=from_second[:],
                 in0=acc[:, :, P:UNIT].unsqueeze(3).to_broadcast(pair_shape),
-                in1=planes[:, tiles, 0:2, :, :].rearrange("p m e h i -> p m (h i) e"),
+                in1=second_table[:, tiles, :, :, :].rearrange("p m h i e -> p m (h i) e"),
                 op=MULT,
             )
             return from_first, from_second
@@ -203,7 +206,6 @@ def tile_mha_pa_kernel(tc, x, freqs_cos, freqs_sin, wqkv, out_0, out_1, out_2):
             return [put_in_order(nc.scalar.copy, raw[:, 0, :]), put_in_order(nc.vector.tensor_copy, raw[:, 1, :])]
 
         gate = const.tile([P, 4], U8)
-        make_planes()
 
         x_grouped = []
         x_mx = []
@@ -212,7 +214,7 @@ def tile_mha_pa_kernel(tc, x, freqs_cos, freqs_sin, wqkv, out_0, out_1, out_2):
         for m in range(TOKEN_TILES):
             if m > 0:
                 x_mx.append(quantise(x_grouped[m - 1], P, const, "x%d" % (m - 1)))
-            grouped = const.tile([P, PASSES * P * PACK], BF16, name="x_grouped%d" % m, align_bytes=64)
+            grouped = x_grouped_pool.tile([P, PASSES * P * PACK], BF16, name="x_grouped", align_bytes=64)
             transpose_tile(
                 x_raw[m][:],
                 None,
@@ -223,6 +225,7 @@ def tile_mha_pa_kernel(tc, x, freqs_cos, freqs_sin, wqkv, out_0, out_1, out_2):
         x_mx.append(quantise(x_grouped[-1], P, const, "x_last"))
         w_grouped = transpose_unit(w_raw[0], [None, None], both)
         w_mx = quantise(w_grouped, UNIT, w_mx_pool, "w")
+        make_tables()
         ordered = [None, None]
 
         result = None

@@ -34,12 +34,13 @@ TOKEN_TILES = S // P
 BANKS = TOKEN_TILES // 2
 STORE_UNITS = 2
 STORE_COLS = STORE_UNITS * UNIT
+UNIT_ORDER = [0, 1, 2, 3, 4, 10, 5, 6, 7, 8, 9, 11]
 LOADS_AHEAD = 6
 STRIDED_UNITS = 2
 
 FLOPS = 2 * S * (Q_DIM + 2 * KV_DIM) * D
 
-assert KV_DIM == STORE_COLS
+assert KV_DIM == STORE_COLS and len(UNIT_ORDER) == W_UNITS
 
 
 def tile_mha_pa_kernel(tc, x, freqs_cos, freqs_sin, wqkv, out_0, out_1, out_2):
@@ -52,7 +53,7 @@ def tile_mha_pa_kernel(tc, x, freqs_cos, freqs_sin, wqkv, out_0, out_1, out_2):
     q_rows = out_0.rearrange("(p m) h d -> p m (h d)", m=TOKEN_TILES)
     k_rows = out_1.rearrange("(p m) h d -> p m (h d)", m=TOKEN_TILES)
     v_rows = out_2.rearrange("(p m) h d -> p m (h d)", m=TOKEN_TILES)
-    store_targets = [q_rows[:, :, c : c + STORE_COLS] for c in range(0, Q_DIM, STORE_COLS)] + [k_rows, v_rows]
+    store_targets = [q_rows[:, :, c : c + STORE_COLS] for c in range(0, Q_DIM, STORE_COLS)] + [k_rows]
 
     with ExitStack() as ctx:
         const = ctx.enter_context(tc.tile_pool(name="const", bufs=1))
@@ -61,8 +62,9 @@ def tile_mha_pa_kernel(tc, x, freqs_cos, freqs_sin, wqkv, out_0, out_1, out_2):
         x_grouped_pool = ctx.enter_context(tc.tile_pool(name="x_grouped", bufs=2))
         grouped_pool = ctx.enter_context(tc.tile_pool(name="grouped", bufs=3))
         w_mx_pool = ctx.enter_context(tc.tile_pool(name="w_mx", bufs=3))
-        product_pool = ctx.enter_context(tc.tile_pool(name="product", bufs=4))
+        product_pool = ctx.enter_context(tc.tile_pool(name="product", bufs=3))
         result_pool = ctx.enter_context(tc.tile_pool(name="result", bufs=3))
+        plain_pool = ctx.enter_context(tc.tile_pool(name="plain", bufs=1))
         flipped_pool = ctx.enter_context(tc.psum_pool(name="flipped", bufs=4))
         acc_pool = ctx.enter_context(tc.psum_pool(name="acc", bufs=2 * BANKS))
         ctx.enter_context(tc.manual_schedule())
@@ -78,12 +80,13 @@ def tile_mha_pa_kernel(tc, x, freqs_cos, freqs_sin, wqkv, out_0, out_1, out_2):
             x_raw.append(raw)
 
         def load_unit(n):
+            unit = UNIT_ORDER[n]
             raw = raw_pool.tile([P, UNIT_TILES, D], BF16, name="w_raw%d" % n)
             if n < STRIDED_UNITS:
                 for j in range(UNIT_TILES):
-                    nc.sync.dma_start(out=raw[:, j, :], in_=w_units[n, :, j, :])
+                    nc.sync.dma_start(out=raw[:, j, :], in_=w_units[unit, :, j, :])
             else:
-                nc.sync.dma_start(out=raw[:], in_=w_units[n, :, :, :])
+                nc.sync.dma_start(out=raw[:], in_=w_units[unit, :, :, :])
             return raw
 
         w_raw = [load_unit(n) for n in range(LOADS_AHEAD)]
@@ -91,17 +94,15 @@ def tile_mha_pa_kernel(tc, x, freqs_cos, freqs_sin, wqkv, out_0, out_1, out_2):
         ident = const.tile([P, P], F32)
         make_identity(nc, ident[:])
 
-        first_table = const.tile([P, TOKEN_TILES, UNIT_HEADS, PAIRS, 2], F32)
-        second_table = const.tile([P, TOKEN_TILES, UNIT_HEADS, PAIRS, 2], F32)
+        planes = const.tile([P, TOKEN_TILES, 3, UNIT_HEADS, PAIRS], BF16)
 
-        def make_tables():
+        def make_planes():
             over_heads = [P, TOKEN_TILES, UNIT_HEADS, PAIRS]
             cos_heads = cos_sb[:].unsqueeze(2).to_broadcast(over_heads)
             sin_heads = sin_sb[:].unsqueeze(2).to_broadcast(over_heads)
-            nc.vector.tensor_copy(out=first_table[:, :, :, :, 0], in_=cos_heads)
-            nc.vector.tensor_copy(out=first_table[:, :, :, :, 1], in_=sin_heads)
-            nc.vector.tensor_scalar_mul(out=second_table[:, :, :, :, 0], in0=sin_heads, scalar1=-1.0)
-            nc.vector.tensor_copy(out=second_table[:, :, :, :, 1], in_=cos_heads)
+            nc.vector.tensor_scalar_mul(out=planes[:, :, 0, :, :], in0=sin_heads, scalar1=-1.0)
+            nc.vector.tensor_copy(out=planes[:, :, 1, :, :], in_=cos_heads)
+            nc.vector.tensor_copy(out=planes[:, :, 2, :, :], in_=sin_heads)
 
         def put_in_order(copy, raw):
             ordered = ordered_pool.tile([P, D], BF16, name="ordered")
@@ -170,20 +171,20 @@ def tile_mha_pa_kernel(tc, x, freqs_cos, freqs_sin, wqkv, out_0, out_1, out_2):
             nc.vector.tensor_tensor(
                 out=from_first[:],
                 in0=acc[:, :, 0:P].unsqueeze(3).to_broadcast(pair_shape),
-                in1=first_table[:, tiles, :, :, :].rearrange("p m h i e -> p m (h i) e"),
+                in1=planes[:, tiles, 1:3, :, :].rearrange("p m e h i -> p m (h i) e"),
                 op=MULT,
             )
             nc.vector.tensor_tensor(
                 out=from_second[:],
                 in0=acc[:, :, P:UNIT].unsqueeze(3).to_broadcast(pair_shape),
-                in1=second_table[:, tiles, :, :, :].rearrange("p m h i e -> p m (h i) e"),
+                in1=planes[:, tiles, 0:2, :, :].rearrange("p m e h i -> p m (h i) e"),
                 op=MULT,
             )
             return from_first, from_second
 
-        def add_products(pair, rotated):
+        def add_products(engine, pair, rotated):
             from_first, from_second = pair
-            nc.gpsimd.tensor_tensor(
+            engine.tensor_tensor(
                 out=rotated,
                 in0=from_first[:].rearrange("p m r e -> p m (r e)"),
                 in1=from_second[:].rearrange("p m r e -> p m (r e)"),
@@ -203,7 +204,8 @@ def tile_mha_pa_kernel(tc, x, freqs_cos, freqs_sin, wqkv, out_0, out_1, out_2):
             raw = w_raw[n]
             if n < STRIDED_UNITS:
                 return [None, None]
-            return [put_in_order(nc.scalar.copy, raw[:, 0, :]), put_in_order(nc.vector.tensor_copy, raw[:, 1, :])]
+            first = put_in_order(nc.scalar.copy, raw[:, 0, :])
+            return [first, put_in_order(nc.scalar.copy, raw[:, 1, :]) if n % 2 == 0 else None]
 
         gate = const.tile([P, 4], U8)
 
@@ -225,12 +227,13 @@ def tile_mha_pa_kernel(tc, x, freqs_cos, freqs_sin, wqkv, out_0, out_1, out_2):
         x_mx.append(quantise(x_grouped[-1], P, const, "x_last"))
         w_grouped = transpose_unit(w_raw[0], [None, None], both)
         w_mx = quantise(w_grouped, UNIT, w_mx_pool, "w")
-        make_tables()
+        make_planes()
         ordered = [None, None]
 
-        result = None
+        results = {}
         late = None
         for n in range(W_UNITS):
+            unit = UNIT_ORDER[n]
             if n + LOADS_AHEAD < W_UNITS:
                 w_raw.append(load_unit(n + LOADS_AHEAD))
             following = n + 1 < W_UNITS
@@ -241,33 +244,31 @@ def tile_mha_pa_kernel(tc, x, freqs_cos, freqs_sin, wqkv, out_0, out_1, out_2):
             banks = [multiply(b, w_mx) for b in range(BANKS)]
             if following:
                 w_mx = quantise(w_grouped, UNIT, w_mx_pool, "w")
-                if late is not None:
-                    hold_gpsimd(w_mx[1])
             if late is not None:
+                if following:
+                    hold_gpsimd(w_mx[1])
                 late()
                 late = None
 
-            part = n % STORE_UNITS
-            if part == 0:
-                result = result_pool.tile([P, TOKEN_TILES, STORE_COLS], F32, name="result")
+            if unit < ROTATED_UNITS:
+                part = unit % STORE_UNITS
+                if part == 0:
+                    results[unit // STORE_UNITS] = result_pool.tile([P, TOKEN_TILES, STORE_COLS], F32, name="result")
+                result = results[unit // STORE_UNITS]
 
-            def finish(b, pair, n=n, result=result):
-                tiles = slice(2 * b, 2 * b + 2)
-                part = n % STORE_UNITS
-                if pair is not None:
-                    add_products(pair, result[:, tiles, part * UNIT : (part + 1) * UNIT])
-                if part == STORE_UNITS - 1:
-                    nc.sync.dma_start(out=store_targets[n // STORE_UNITS][:, tiles, :], in_=result[:, tiles, :])
+                def finish(b, engine, pair, unit=unit, part=part, result=result):
+                    tiles = slice(2 * b, 2 * b + 2)
+                    add_products(engine, pair, result[:, tiles, part * UNIT : (part + 1) * UNIT])
+                    if part == STORE_UNITS - 1:
+                        nc.sync.dma_start(out=store_targets[unit // STORE_UNITS][:, tiles, :], in_=result[:, tiles, :])
 
-            if n < ROTATED_UNITS:
-                finish(0, products(banks[0], slice(0, 2)))
-                pair = products(banks[1], slice(2, 4))
-                late = lambda finish=finish, pair=pair: finish(1, pair)
+                pair = products(banks[0], slice(0, 2))
+                late = lambda finish=finish, pair=pair: finish(0, nc.gpsimd, pair)
+                finish(1, nc.vector, products(banks[1], slice(2, 4)))
             else:
+                part = unit - ROTATED_UNITS
+                plain = plain_pool.tile([P, TOKEN_TILES, UNIT], F32, name="plain")
                 for b in range(BANKS):
-                    interleave(
-                        [nc.scalar.copy, nc.vector.tensor_copy][b],
-                        banks[b],
-                        result[:, 2 * b : 2 * b + 2, part * UNIT : (part + 1) * UNIT],
-                    )
-                    finish(b, None)
+                    tiles = slice(2 * b, 2 * b + 2)
+                    interleave(nc.scalar.copy, banks[b], plain[:, tiles, :])
+                    nc.sync.dma_start(out=v_rows[:, tiles, part * UNIT : (part + 1) * UNIT], in_=plain[:, tiles, :])

@@ -34,13 +34,13 @@ TOKEN_TILES = S // P
 BANKS = TOKEN_TILES // 2
 STORE_UNITS = 2
 STORE_COLS = STORE_UNITS * UNIT
-UNIT_ORDER = [0, 1, 2, 3, 4, 10, 5, 6, 7, 8, 9, 11]
+ORDER_AHEAD = 3
 LOADS_AHEAD = 6
 STRIDED_UNITS = 2
 
 FLOPS = 2 * S * (Q_DIM + 2 * KV_DIM) * D
 
-assert KV_DIM == STORE_COLS and len(UNIT_ORDER) == W_UNITS
+assert KV_DIM == STORE_COLS
 
 
 def tile_mha_pa_kernel(tc, x, freqs_cos, freqs_sin, wqkv, out_0, out_1, out_2):
@@ -53,7 +53,7 @@ def tile_mha_pa_kernel(tc, x, freqs_cos, freqs_sin, wqkv, out_0, out_1, out_2):
     q_rows = out_0.rearrange("(p m) h d -> p m (h d)", m=TOKEN_TILES)
     k_rows = out_1.rearrange("(p m) h d -> p m (h d)", m=TOKEN_TILES)
     v_rows = out_2.rearrange("(p m) h d -> p m (h d)", m=TOKEN_TILES)
-    store_targets = [q_rows[:, :, c : c + STORE_COLS] for c in range(0, Q_DIM, STORE_COLS)] + [k_rows]
+    store_targets = [q_rows[:, :, c : c + STORE_COLS] for c in range(0, Q_DIM, STORE_COLS)] + [k_rows, v_rows]
 
     with ExitStack() as ctx:
         const = ctx.enter_context(tc.tile_pool(name="const", bufs=1))
@@ -64,7 +64,6 @@ def tile_mha_pa_kernel(tc, x, freqs_cos, freqs_sin, wqkv, out_0, out_1, out_2):
         w_mx_pool = ctx.enter_context(tc.tile_pool(name="w_mx", bufs=3))
         product_pool = ctx.enter_context(tc.tile_pool(name="product", bufs=3))
         result_pool = ctx.enter_context(tc.tile_pool(name="result", bufs=3))
-        plain_pool = ctx.enter_context(tc.tile_pool(name="plain", bufs=1))
         flipped_pool = ctx.enter_context(tc.psum_pool(name="flipped", bufs=4))
         acc_pool = ctx.enter_context(tc.psum_pool(name="acc", bufs=2 * BANKS))
         ctx.enter_context(tc.manual_schedule())
@@ -80,13 +79,12 @@ def tile_mha_pa_kernel(tc, x, freqs_cos, freqs_sin, wqkv, out_0, out_1, out_2):
             x_raw.append(raw)
 
         def load_unit(n):
-            unit = UNIT_ORDER[n]
             raw = raw_pool.tile([P, UNIT_TILES, D], BF16, name="w_raw%d" % n)
             if n < STRIDED_UNITS:
                 for j in range(UNIT_TILES):
-                    nc.sync.dma_start(out=raw[:, j, :], in_=w_units[unit, :, j, :])
+                    nc.sync.dma_start(out=raw[:, j, :], in_=w_units[n, :, j, :])
             else:
-                nc.sync.dma_start(out=raw[:], in_=w_units[unit, :, :, :])
+                nc.sync.dma_start(out=raw[:], in_=w_units[n, :, :, :])
             return raw
 
         w_raw = [load_unit(n) for n in range(LOADS_AHEAD)]
@@ -94,15 +92,16 @@ def tile_mha_pa_kernel(tc, x, freqs_cos, freqs_sin, wqkv, out_0, out_1, out_2):
         ident = const.tile([P, P], F32)
         make_identity(nc, ident[:])
 
-        planes = const.tile([P, TOKEN_TILES, 3, UNIT_HEADS, PAIRS], BF16)
+        factors = const.tile([P, TOKEN_TILES, 2, UNIT_TILES, UNIT_HEADS, PAIRS], BF16)
 
-        def make_planes():
+        def make_factors():
             over_heads = [P, TOKEN_TILES, UNIT_HEADS, PAIRS]
             cos_heads = cos_sb[:].unsqueeze(2).to_broadcast(over_heads)
             sin_heads = sin_sb[:].unsqueeze(2).to_broadcast(over_heads)
-            nc.vector.tensor_scalar_mul(out=planes[:, :, 0, :, :], in0=sin_heads, scalar1=-1.0)
-            nc.vector.tensor_copy(out=planes[:, :, 1, :, :], in_=cos_heads)
-            nc.vector.tensor_copy(out=planes[:, :, 2, :, :], in_=sin_heads)
+            nc.vector.tensor_copy(out=factors[:, :, 0, 0, :, :], in_=cos_heads)
+            nc.vector.tensor_copy(out=factors[:, :, 1, 0, :, :], in_=sin_heads)
+            nc.vector.tensor_scalar_mul(out=factors[:, :, 0, 1, :, :], in0=sin_heads, scalar1=-1.0)
+            nc.vector.tensor_copy(out=factors[:, :, 1, 1, :, :], in_=cos_heads)
 
         def put_in_order(copy, raw):
             ordered = ordered_pool.tile([P, D], BF16, name="ordered")
@@ -128,23 +127,16 @@ def tile_mha_pa_kernel(tc, x, freqs_cos, freqs_sin, wqkv, out_0, out_1, out_2):
                     out=target[:, first : first + BANK_PASSES, :, :], in_=flipped[:].rearrange("p b u r -> p b r u")
                 )
 
-        def transpose_unit(raw, ordered, copies):
-            grouped = grouped_pool.tile([P, PASSES * UNIT * PACK], BF16, name="grouped", align_bytes=64)
-            words = grouped[:].bitcast(F32).rearrange(
-                "p (g j r u) -> p g j r u", g=PASSES, j=UNIT_TILES, u=WORD_HALVES
-            )
-            for j in range(UNIT_TILES):
-                transpose_tile(raw[:, j, :], ordered[j], words[:, :, j, :, :], copies)
-            return grouped
-
-        def quantise(grouped, rows, pool, name):
+        def quantise(grouped, rows, pool, name, calls=1):
             codes = pool.tile([P, PASSES, rows], U32, name=name + "_codes", align_bytes=64)
             scales = pool.tile([P, PASSES, rows], U8, name=name + "_scales", align_bytes=64)
-            nc.vector.quantize_mx(
-                out=codes[:].rearrange("p g c -> p (g c)").bitcast(FP8X4),
-                scales=scales[:].rearrange("p g c -> p (g c)"),
-                in_=grouped[:],
-            )
+            for c in range(calls):
+                cols = slice(c * PASSES * rows // calls, (c + 1) * PASSES * rows // calls)
+                nc.vector.quantize_mx(
+                    out=codes[:].rearrange("p g c -> p (g c)")[:, cols].bitcast(FP8X4),
+                    scales=scales[:].rearrange("p g c -> p (g c)")[:, cols],
+                    in_=grouped[:, PACK * cols.start : PACK * cols.stop],
+                )
             return codes, scales
 
         def multiply(b, w_unit):
@@ -165,29 +157,21 @@ def tile_mha_pa_kernel(tc, x, freqs_cos, freqs_sin, wqkv, out_0, out_1, out_2):
             return acc
 
         def products(acc, tiles):
-            pair_shape = [P, 2, P, 2]
-            from_first = product_pool.tile(pair_shape, F32, name="from_first")
-            from_second = product_pool.tile(pair_shape, F32, name="from_second")
+            shape = [P, 2, UNIT, 2]
+            product = product_pool.tile(shape, F32, name="product")
             nc.vector.tensor_tensor(
-                out=from_first[:],
-                in0=acc[:, :, 0:P].unsqueeze(3).to_broadcast(pair_shape),
-                in1=planes[:, tiles, 1:3, :, :].rearrange("p m e h i -> p m (h i) e"),
+                out=product[:],
+                in0=acc[:].unsqueeze(3).to_broadcast(shape),
+                in1=factors[:, tiles, :, :, :, :].rearrange("p m e j h i -> p m (j h i) e"),
                 op=MULT,
             )
-            nc.vector.tensor_tensor(
-                out=from_second[:],
-                in0=acc[:, :, P:UNIT].unsqueeze(3).to_broadcast(pair_shape),
-                in1=planes[:, tiles, 0:2, :, :].rearrange("p m e h i -> p m (h i) e"),
-                op=MULT,
-            )
-            return from_first, from_second
+            return product
 
-        def add_products(engine, pair, rotated):
-            from_first, from_second = pair
+        def add_products(engine, product, rotated):
             engine.tensor_tensor(
                 out=rotated,
-                in0=from_first[:].rearrange("p m r e -> p m (r e)"),
-                in1=from_second[:].rearrange("p m r e -> p m (r e)"),
+                in0=product[:, :, 0:P, :].rearrange("p m r e -> p m (r e)"),
+                in1=product[:, :, P:UNIT, :].rearrange("p m r e -> p m (r e)"),
                 op=ADD,
             )
 
@@ -200,47 +184,66 @@ def tile_mha_pa_kernel(tc, x, freqs_cos, freqs_sin, wqkv, out_0, out_1, out_2):
                 in_=acc[:].rearrange("p m (j r) -> p m r j", j=UNIT_TILES),
             )
 
-        def put_unit_in_order(n):
-            raw = w_raw[n]
-            if n < STRIDED_UNITS:
-                return [None, None]
-            first = put_in_order(nc.scalar.copy, raw[:, 0, :])
-            return [first, put_in_order(nc.scalar.copy, raw[:, 1, :]) if n % 2 == 0 else None]
+        ordered = {(n, j): None for n in range(W_UNITS) for j in range(UNIT_TILES)}
+
+        def order_tile(n, j, copy):
+            ordered[n, j] = put_in_order(copy, w_raw[n][:, j, :])
+
+        def new_grouped():
+            return grouped_pool.tile([P, PASSES * UNIT * PACK], BF16, name="grouped", align_bytes=64)
+
+        def transpose_tile_of_unit(n, j, grouped, copies):
+            words = grouped[:].bitcast(F32).rearrange(
+                "p (g j r u) -> p g j r u", g=PASSES, j=UNIT_TILES, u=WORD_HALVES
+            )
+            transpose_tile(w_raw[n][:, j, :], ordered[n, j], words[:, :, j, :, :], copies)
 
         gate = const.tile([P, 4], U8)
+        make_factors()
 
+        alone = [nc.scalar.copy, nc.scalar.copy]
+        both = [nc.scalar.copy, nc.vector.tensor_copy]
         x_grouped = []
         x_mx = []
-        both = [nc.scalar.copy, nc.vector.tensor_copy]
-        alone = [nc.scalar.copy, nc.scalar.copy]
-        for m in range(TOKEN_TILES):
-            if m > 0:
-                x_mx.append(quantise(x_grouped[m - 1], P, const, "x%d" % (m - 1)))
-            grouped = x_grouped_pool.tile([P, PASSES * P * PACK], BF16, name="x_grouped", align_bytes=64)
-            transpose_tile(
-                x_raw[m][:],
-                None,
-                grouped[:].bitcast(F32).rearrange("p (g r u) -> p g r u", g=PASSES, u=WORD_HALVES),
-                [alone, both][m % 2],
-            )
-            x_grouped.append(grouped)
-        x_mx.append(quantise(x_grouped[-1], P, const, "x_last"))
-        w_grouped = transpose_unit(w_raw[0], [None, None], both)
-        w_mx = quantise(w_grouped, UNIT, w_mx_pool, "w")
-        make_planes()
-        ordered = [None, None]
 
-        results = {}
+        def transpose_x(m):
+            grouped = x_grouped_pool.tile([P, PASSES * P * PACK], BF16, name="x_grouped", align_bytes=64)
+            words = grouped[:].bitcast(F32).rearrange("p (g r u) -> p g r u", g=PASSES, u=WORD_HALVES)
+            transpose_tile(x_raw[m][:], None, words, alone)
+            x_grouped.append(grouped)
+
+        def quantise_x(m):
+            x_mx.append(quantise(x_grouped[m], P, const, "x%d" % m))
+
+        transpose_x(0)
+        transpose_x(1)
+        quantise_x(0)
+        transpose_x(2)
+        quantise_x(1)
+        order_tile(0, 0, nc.vector.tensor_copy)
+        transpose_x(3)
+        quantise_x(2)
+        order_tile(0, 1, nc.vector.tensor_copy)
+        w_grouped = new_grouped()
+        transpose_tile_of_unit(0, 0, w_grouped, both)
+        quantise_x(3)
+        transpose_tile_of_unit(0, 1, w_grouped, both)
+        w_mx = quantise(w_grouped, UNIT, w_mx_pool, "w", calls=2)
+        for n in range(STRIDED_UNITS, ORDER_AHEAD):
+            order_tile(n, 0, nc.scalar.copy)
+
+        result = None
         late = None
         for n in range(W_UNITS):
-            unit = UNIT_ORDER[n]
             if n + LOADS_AHEAD < W_UNITS:
                 w_raw.append(load_unit(n + LOADS_AHEAD))
             following = n + 1 < W_UNITS
             if following:
-                w_grouped = transpose_unit(w_raw[n + 1], ordered, alone)
-            if n + 2 < W_UNITS:
-                ordered = put_unit_in_order(n + 2)
+                w_grouped = new_grouped()
+                for j in range(UNIT_TILES):
+                    transpose_tile_of_unit(n + 1, j, w_grouped, alone)
+            if n + ORDER_AHEAD < W_UNITS:
+                order_tile(n + ORDER_AHEAD, 0, nc.scalar.copy)
             banks = [multiply(b, w_mx) for b in range(BANKS)]
             if following:
                 w_mx = quantise(w_grouped, UNIT, w_mx_pool, "w")
@@ -250,25 +253,27 @@ def tile_mha_pa_kernel(tc, x, freqs_cos, freqs_sin, wqkv, out_0, out_1, out_2):
                 late()
                 late = None
 
-            if unit < ROTATED_UNITS:
-                part = unit % STORE_UNITS
-                if part == 0:
-                    results[unit // STORE_UNITS] = result_pool.tile([P, TOKEN_TILES, STORE_COLS], F32, name="result")
-                result = results[unit // STORE_UNITS]
+            part = n % STORE_UNITS
+            if part == 0:
+                result = result_pool.tile([P, TOKEN_TILES, STORE_COLS], F32, name="result")
 
-                def finish(b, engine, pair, unit=unit, part=part, result=result):
+            def target(b, result=result, part=part):
+                return result[:, 2 * b : 2 * b + 2, part * UNIT : (part + 1) * UNIT]
+
+            def store(b, n=n, result=result, part=part):
+                if part == STORE_UNITS - 1:
                     tiles = slice(2 * b, 2 * b + 2)
-                    add_products(engine, pair, result[:, tiles, part * UNIT : (part + 1) * UNIT])
-                    if part == STORE_UNITS - 1:
-                        nc.sync.dma_start(out=store_targets[unit // STORE_UNITS][:, tiles, :], in_=result[:, tiles, :])
+                    nc.sync.dma_start(out=store_targets[n // STORE_UNITS][:, tiles, :], in_=result[:, tiles, :])
 
-                pair = products(banks[0], slice(0, 2))
-                late = lambda finish=finish, pair=pair: finish(0, nc.gpsimd, pair)
-                finish(1, nc.vector, products(banks[1], slice(2, 4)))
+            if n < ROTATED_UNITS:
+                pair = [products(banks[b], slice(2 * b, 2 * b + 2)) for b in range(BANKS)]
+                add_products(nc.vector, pair[0], target(0))
+                store(0)
+
+                def late(product=pair[1], target=target, store=store):
+                    add_products(nc.gpsimd, product, target(1))
+                    store(1)
             else:
-                part = unit - ROTATED_UNITS
-                plain = plain_pool.tile([P, TOKEN_TILES, UNIT], F32, name="plain")
                 for b in range(BANKS):
-                    tiles = slice(2 * b, 2 * b + 2)
-                    interleave(nc.scalar.copy, banks[b], plain[:, tiles, :])
-                    nc.sync.dma_start(out=v_rows[:, tiles, part * UNIT : (part + 1) * UNIT], in_=plain[:, tiles, :])
+                    interleave(nc.scalar.copy, banks[b], target(b))
+                    store(b)

@@ -35,6 +35,7 @@ BANKS = TOKEN_TILES // 2
 STORE_UNITS = 2
 STORE_COLS = STORE_UNITS * UNIT
 ORDER_AHEAD = 3
+SCALAR_ORDERS = (5, 8, 11)
 LOADS_AHEAD = 6
 STRIDED_UNITS = 2
 
@@ -53,17 +54,18 @@ def tile_mha_pa_kernel(tc, x, freqs_cos, freqs_sin, wqkv, out_0, out_1, out_2):
     q_rows = out_0.rearrange("(p m) h d -> p m (h d)", m=TOKEN_TILES)
     k_rows = out_1.rearrange("(p m) h d -> p m (h d)", m=TOKEN_TILES)
     v_rows = out_2.rearrange("(p m) h d -> p m (h d)", m=TOKEN_TILES)
-    store_targets = [q_rows[:, :, c : c + STORE_COLS] for c in range(0, Q_DIM, STORE_COLS)] + [k_rows, v_rows]
+    store_targets = [q_rows[:, :, c : c + STORE_COLS] for c in range(0, Q_DIM, STORE_COLS)] + [k_rows]
 
     with ExitStack() as ctx:
         const = ctx.enter_context(tc.tile_pool(name="const", bufs=1))
         raw_pool = ctx.enter_context(tc.tile_pool(name="raw", bufs=1))
-        ordered_pool = ctx.enter_context(tc.tile_pool(name="ordered", bufs=4))
+        ordered_pool = ctx.enter_context(tc.tile_pool(name="ordered", bufs=5))
         x_grouped_pool = ctx.enter_context(tc.tile_pool(name="x_grouped", bufs=2))
         grouped_pool = ctx.enter_context(tc.tile_pool(name="grouped", bufs=3))
         w_mx_pool = ctx.enter_context(tc.tile_pool(name="w_mx", bufs=3))
         product_pool = ctx.enter_context(tc.tile_pool(name="product", bufs=3))
-        result_pool = ctx.enter_context(tc.tile_pool(name="result", bufs=3))
+        result_pool = ctx.enter_context(tc.tile_pool(name="result", bufs=2))
+        plain_pool = ctx.enter_context(tc.tile_pool(name="plain", bufs=2))
         flipped_pool = ctx.enter_context(tc.psum_pool(name="flipped", bufs=4))
         acc_pool = ctx.enter_context(tc.psum_pool(name="acc", bufs=2 * BANKS))
         ctx.enter_context(tc.manual_schedule())
@@ -74,9 +76,12 @@ def tile_mha_pa_kernel(tc, x, freqs_cos, freqs_sin, wqkv, out_0, out_1, out_2):
         nc.scalar.dma_start(out=sin_sb[:], in_=sin_rows)
         x_raw = []
         for m in range(TOKEN_TILES):
-            raw = raw_pool.tile([P, D], BF16, name="x_raw%d" % m)
-            nc.sync.dma_start(out=raw[:], in_=x_rows[m, :, :])
-            x_raw.append(raw)
+            pieces = 2 if m == 0 else 1
+            x_raw.append([])
+            for c in range(pieces):
+                raw = raw_pool.tile([P, D // pieces], BF16, name="x_raw%d_%d" % (m, c))
+                nc.sync.dma_start(out=raw[:], in_=x_rows[m, :, c * D // pieces : (c + 1) * D // pieces])
+                x_raw[m].append(raw[:])
 
         def load_unit(n):
             raw = raw_pool.tile([P, UNIT_TILES, D], BF16, name="w_raw%d" % n)
@@ -111,14 +116,16 @@ def tile_mha_pa_kernel(tc, x, freqs_cos, freqs_sin, wqkv, out_0, out_1, out_2):
             )
             return ordered
 
-        def transpose_tile(raw, ordered, target, copies):
-            words = raw.bitcast(F32) if ordered is None else ordered[:].bitcast(F32)
+        def transpose_tile(pieces, is_ordered, target, copies):
+            piece_words = WORDS // len(pieces)
             for first, copy in zip(range(0, PASSES, BANK_PASSES), copies):
                 flipped = flipped_pool.tile([P, BANK_PASSES, WORD_HALVES, P], F32, name="flipped")
                 for b in range(BANK_PASSES):
                     for u in range(WORD_HALVES):
-                        start = (first + b) * WORD_HALVES * P
-                        if ordered is None:
+                        place = (first + b) * WORD_HALVES * P
+                        words = pieces[place // piece_words].bitcast(F32)
+                        start = place % piece_words
+                        if not is_ordered:
                             cols = words[:, start + u : start + WORD_HALVES * P : WORD_HALVES]
                         else:
                             cols = words[:, start + u * P : start + (u + 1) * P]
@@ -139,11 +146,11 @@ def tile_mha_pa_kernel(tc, x, freqs_cos, freqs_sin, wqkv, out_0, out_1, out_2):
                 )
             return codes, scales
 
-        def multiply(b, w_unit):
+        def multiply(token_tiles, w_unit):
             w_codes, w_scales = w_unit
             acc = acc_pool.tile([P, 2, UNIT], F32, name="acc")
-            for j in range(2):
-                x_codes, x_scales = x_mx[2 * b + j]
+            for j, m in enumerate(token_tiles):
+                x_codes, x_scales = x_mx[m]
                 for g in range(PASSES):
                     nc.tensor.matmul_mx(
                         out=acc[:, j, :],
@@ -178,16 +185,22 @@ def tile_mha_pa_kernel(tc, x, freqs_cos, freqs_sin, wqkv, out_0, out_1, out_2):
         def hold_gpsimd(scales):
             nc.gpsimd.tensor_copy(out=gate[:], in_=scales[:, 0, 0:4])
 
-        def interleave(copy, acc, plain):
+        def interleave(copy, sums, plain):
             copy(
-                out=plain.rearrange("p m (r j) -> p m r j", j=UNIT_TILES),
-                in_=acc[:].rearrange("p m (j r) -> p m r j", j=UNIT_TILES),
+                out=plain.rearrange("p (r j) -> p r j", j=UNIT_TILES),
+                in_=sums.rearrange("p (j r) -> p r j", j=UNIT_TILES),
             )
 
         ordered = {(n, j): None for n in range(W_UNITS) for j in range(UNIT_TILES)}
 
         def order_tile(n, j, copy):
             ordered[n, j] = put_in_order(copy, w_raw[n][:, j, :])
+
+        def order_unit(n):
+            if n < W_UNITS:
+                order_tile(n, 0, nc.scalar.copy)
+                if n in SCALAR_ORDERS:
+                    order_tile(n, 1, nc.scalar.copy)
 
         def new_grouped():
             return grouped_pool.tile([P, PASSES * UNIT * PACK], BF16, name="grouped", align_bytes=64)
@@ -196,7 +209,8 @@ def tile_mha_pa_kernel(tc, x, freqs_cos, freqs_sin, wqkv, out_0, out_1, out_2):
             words = grouped[:].bitcast(F32).rearrange(
                 "p (g j r u) -> p g j r u", g=PASSES, j=UNIT_TILES, u=WORD_HALVES
             )
-            transpose_tile(w_raw[n][:, j, :], ordered[n, j], words[:, :, j, :, :], copies)
+            source = w_raw[n][:, j, :] if ordered[n, j] is None else ordered[n, j][:]
+            transpose_tile([source], ordered[n, j] is not None, words[:, :, j, :, :], copies)
 
         gate = const.tile([P, 4], U8)
         make_factors()
@@ -209,7 +223,7 @@ def tile_mha_pa_kernel(tc, x, freqs_cos, freqs_sin, wqkv, out_0, out_1, out_2):
         def transpose_x(m):
             grouped = x_grouped_pool.tile([P, PASSES * P * PACK], BF16, name="x_grouped", align_bytes=64)
             words = grouped[:].bitcast(F32).rearrange("p (g r u) -> p g r u", g=PASSES, u=WORD_HALVES)
-            transpose_tile(x_raw[m][:], None, words, alone)
+            transpose_tile(x_raw[m], False, words, alone)
             x_grouped.append(grouped)
 
         def quantise_x(m):
@@ -220,20 +234,18 @@ def tile_mha_pa_kernel(tc, x, freqs_cos, freqs_sin, wqkv, out_0, out_1, out_2):
         quantise_x(0)
         transpose_x(2)
         quantise_x(1)
-        order_tile(0, 0, nc.vector.tensor_copy)
         transpose_x(3)
         quantise_x(2)
-        order_tile(0, 1, nc.vector.tensor_copy)
         w_grouped = new_grouped()
         transpose_tile_of_unit(0, 0, w_grouped, both)
         quantise_x(3)
         transpose_tile_of_unit(0, 1, w_grouped, both)
         w_mx = quantise(w_grouped, UNIT, w_mx_pool, "w", calls=2)
-        for n in range(STRIDED_UNITS, ORDER_AHEAD):
-            order_tile(n, 0, nc.scalar.copy)
+        order_tile(STRIDED_UNITS, 0, nc.vector.tensor_copy)
 
         result = None
         late = None
+        held = None
         for n in range(W_UNITS):
             if n + LOADS_AHEAD < W_UNITS:
                 w_raw.append(load_unit(n + LOADS_AHEAD))
@@ -242,11 +254,14 @@ def tile_mha_pa_kernel(tc, x, freqs_cos, freqs_sin, wqkv, out_0, out_1, out_2):
                 w_grouped = new_grouped()
                 for j in range(UNIT_TILES):
                     transpose_tile_of_unit(n + 1, j, w_grouped, alone)
-            if n + ORDER_AHEAD < W_UNITS:
-                order_tile(n + ORDER_AHEAD, 0, nc.scalar.copy)
-            banks = [multiply(b, w_mx) for b in range(BANKS)]
+            order_unit(n + ORDER_AHEAD)
+            step = 2 if following else 1
+            banks = [multiply(range(m, m + step), w_mx) for m in range(0, TOKEN_TILES, step)]
             if following:
                 w_mx = quantise(w_grouped, UNIT, w_mx_pool, "w")
+            if held is not None:
+                held()
+                held = None
             if late is not None:
                 if following:
                     hold_gpsimd(w_mx[1])
@@ -254,26 +269,39 @@ def tile_mha_pa_kernel(tc, x, freqs_cos, freqs_sin, wqkv, out_0, out_1, out_2):
                 late = None
 
             part = n % STORE_UNITS
-            if part == 0:
+            if part == 0 and n < ROTATED_UNITS:
                 result = result_pool.tile([P, TOKEN_TILES, STORE_COLS], F32, name="result")
 
             def target(b, result=result, part=part):
                 return result[:, 2 * b : 2 * b + 2, part * UNIT : (part + 1) * UNIT]
 
             def store(b, n=n, result=result, part=part):
-                if part == STORE_UNITS - 1:
-                    tiles = slice(2 * b, 2 * b + 2)
-                    nc.sync.dma_start(out=store_targets[n // STORE_UNITS][:, tiles, :], in_=result[:, tiles, :])
+                tiles = slice(2 * b, 2 * b + 2)
+                stores = store_targets[n // STORE_UNITS]
+                if n >= ROTATED_UNITS - STORE_UNITS:
+                    cols = slice(part * UNIT, (part + 1) * UNIT)
+                    nc.sync.dma_start(out=stores[:, tiles, cols], in_=result[:, tiles, cols])
+                elif part == STORE_UNITS - 1:
+                    nc.sync.dma_start(out=stores[:, tiles, :], in_=result[:, tiles, :])
 
             if n < ROTATED_UNITS:
                 pair = [products(banks[b], slice(2 * b, 2 * b + 2)) for b in range(BANKS)]
-                add_products(nc.vector, pair[0], target(0))
-                store(0)
+                if n == ROTATED_UNITS - 1:
+                    def held(pair=pair, target=target, store=store):
+                        for b in range(BANKS):
+                            add_products(nc.vector, pair[b], target(b))
+                            store(b)
 
-                def late(product=pair[1], target=target, store=store):
-                    add_products(nc.gpsimd, product, target(1))
-                    store(1)
+                else:
+                    add_products(nc.vector, pair[0], target(0))
+                    store(0)
+
+                    def late(product=pair[1], target=target, store=store):
+                        add_products(nc.gpsimd, product, target(1))
+                        store(1)
             else:
-                for b in range(BANKS):
-                    interleave(nc.scalar.copy, banks[b], target(b))
-                    store(b)
+                plain = plain_pool.tile([P, TOKEN_TILES, UNIT], F32, name="plain")
+                helper = nc.scalar.copy if following else nc.vector.tensor_copy
+                for m in range(TOKEN_TILES):
+                    interleave(helper if m % 2 else nc.scalar.copy, banks[m // step][:, m % step, :], plain[:, m, :])
+                    nc.sync.dma_start(out=v_rows[:, m, part * UNIT : (part + 1) * UNIT], in_=plain[:, m, :])

@@ -25,6 +25,8 @@ PASSES = D // K_PASS
 WORD_HALVES = 2
 WORDS = D // 2
 BANK_PASSES = 2
+BANK_COLS = BANK_PASSES * WORD_HALVES * P
+WARM_UP_MATMULS = 4
 UNIT = 256
 UNIT_TILES = UNIT // P
 W_UNITS = (Q_DIM + 2 * KV_DIM) // UNIT
@@ -75,7 +77,8 @@ def tile_mha_pa_kernel(tc, x, freqs_cos, freqs_sin, wqkv, out_0, out_1, out_2):
         nc.scalar.dma_start(out=cos_sb[:], in_=cos_rows)
         nc.scalar.dma_start(out=sin_sb[:], in_=sin_rows)
         x_raw = []
-        for m in range(TOKEN_TILES):
+
+        def load_x(m):
             pieces = 2 if m == 0 else 1
             x_raw.append([])
             for c in range(pieces):
@@ -92,7 +95,20 @@ def tile_mha_pa_kernel(tc, x, freqs_cos, freqs_sin, wqkv, out_0, out_1, out_2):
                 nc.sync.dma_start(out=raw[:], in_=w_units[n, :, :, :])
             return raw
 
-        w_raw = [load_unit(n) for n in range(LOADS_AHEAD)]
+        load_x(0)
+        load_x(1)
+        w_raw = [load_unit(0)]
+        load_x(2)
+        load_x(3)
+        w_raw += [load_unit(n) for n in range(1, LOADS_AHEAD)]
+
+        idle = const.tile([P, BANK_COLS], BF16)
+        nc.vector.memset(idle[:], 0.0)
+        unused = flipped_pool.tile([P, BANK_PASSES, WORD_HALVES, P], F32, name="flipped")
+        for i in range(WARM_UP_MATMULS):
+            nc.tensor.matmul(
+                out=unused[:].rearrange("p b u r -> p (b u r)"), lhsT=idle[:, 0:P], rhs=idle[:], start=True, stop=True
+            )
 
         ident = const.tile([P, P], F32)
         make_identity(nc, ident[:])
@@ -232,15 +248,16 @@ def tile_mha_pa_kernel(tc, x, freqs_cos, freqs_sin, wqkv, out_0, out_1, out_2):
         transpose_x(0)
         transpose_x(1)
         quantise_x(0)
-        transpose_x(2)
-        quantise_x(1)
-        transpose_x(3)
-        quantise_x(2)
         w_grouped = new_grouped()
         transpose_tile_of_unit(0, 0, w_grouped, both)
-        quantise_x(3)
+        quantise_x(1)
         transpose_tile_of_unit(0, 1, w_grouped, both)
+        transpose_x(2)
         w_mx = quantise(w_grouped, UNIT, w_mx_pool, "w", calls=2)
+        first_bank = multiply(range(2), w_mx)
+        transpose_x(3)
+        quantise_x(2)
+        quantise_x(3)
         order_tile(STRIDED_UNITS, 0, nc.vector.tensor_copy)
 
         result = None
@@ -256,7 +273,10 @@ def tile_mha_pa_kernel(tc, x, freqs_cos, freqs_sin, wqkv, out_0, out_1, out_2):
                     transpose_tile_of_unit(n + 1, j, w_grouped, alone)
             order_unit(n + ORDER_AHEAD)
             step = 2 if following else 1
-            banks = [multiply(range(m, m + step), w_mx) for m in range(0, TOKEN_TILES, step)]
+            starts = range(0 if n > 0 else step, TOKEN_TILES, step)
+            banks = [multiply(range(m, m + step), w_mx) for m in starts]
+            if n == 0:
+                banks = [first_bank] + banks
             if following:
                 w_mx = quantise(w_grouped, UNIT, w_mx_pool, "w")
             if held is not None:

from contextlib import ExitStack

import concourse.mybir as mybir
from concourse.masks import make_identity

F32 = mybir.dt.float32
BF16 = mybir.dt.bfloat16
U32 = mybir.dt.uint32
U8 = mybir.dt.uint8
FP8X4 = mybir.dt.float8_e4m3fn_x4
MULT = mybir.AluOpType.mult
ADD = mybir.AluOpType.add

P = 128
S = 512
D = 2048
Q_DIM = 2048
KV_DIM = 512
HEAD_DIM = 128
PAIRS = HEAD_DIM // 2

PACK = 4
K_PASS = P * PACK
PASSES = D // K_PASS
WORD_HALVES = 2
WORDS = D // 2
BANK_PASSES = 2
BANK_COLS = BANK_PASSES * WORD_HALVES * P
WARM_UP_MATMULS = 4
UNIT = 256
UNIT_TILES = UNIT // P
W_UNITS = (Q_DIM + 2 * KV_DIM) // UNIT
ROTATED_UNITS = (Q_DIM + KV_DIM) // UNIT
UNIT_HEADS = UNIT // HEAD_DIM
TOKEN_TILES = S // P
BANKS = TOKEN_TILES // 2
STORE_UNITS = 2
STORE_COLS = STORE_UNITS * UNIT
ORDER_AHEAD = 3
SCALAR_ORDERS = (5, 8, 11)
LOADS_AHEAD = 6
STRIDED_UNITS = 2

FLOPS = 2 * S * (Q_DIM + 2 * KV_DIM) * D

assert KV_DIM == STORE_COLS


def tile_mha_pa_kernel(tc, x, freqs_cos, freqs_sin, wqkv, out_0, out_1, out_2):
    nc = tc.nc

    x_rows = x.rearrange("(p m) k -> m p k", m=TOKEN_TILES)
    cos_rows = freqs_cos.rearrange("(p m) i -> p m i", m=TOKEN_TILES)
    sin_rows = freqs_sin.rearrange("(p m) i -> p m i", m=TOKEN_TILES)
    w_units = wqkv.rearrange("(n p j) k -> n p j k", p=P, j=UNIT_TILES)
    q_rows = out_0.rearrange("(p m) h d -> p m (h d)", m=TOKEN_TILES)
    k_rows = out_1.rearrange("(p m) h d -> p m (h d)", m=TOKEN_TILES)
    v_rows = out_2.rearrange("(p m) h d -> p m (h d)", m=TOKEN_TILES)
    store_targets = [q_rows[:, :, c : c + STORE_COLS] for c in range(0, Q_DIM, STORE_COLS)] + [k_rows]

    with ExitStack() as ctx:
        const = ctx.enter_context(tc.tile_pool(name="const", bufs=1))
        raw_pool = ctx.enter_context(tc.tile_pool(name="raw", bufs=1))
        ordered_pool = ctx.enter_context(tc.tile_pool(name="ordered", bufs=5))
        x_grouped_pool = ctx.enter_context(tc.tile_pool(name="x_grouped", bufs=2))
        grouped_pool = ctx.enter_context(tc.tile_pool(name="grouped", bufs=3))
        w_mx_pool = ctx.enter_context(tc.tile_pool(name="w_mx", bufs=3))
        product_pool = ctx.enter_context(tc.tile_pool(name="product", bufs=3))
        result_pool = ctx.enter_context(tc.tile_pool(name="result", bufs=2))
        plain_pool = ctx.enter_context(tc.tile_pool(name="plain", bufs=2))
        flipped_pool = ctx.enter_context(tc.psum_pool(name="flipped", bufs=4))
        acc_pool = ctx.enter_context(tc.psum_pool(name="acc", bufs=2 * BANKS))
        ctx.enter_context(tc.manual_schedule())

        cos_sb = const.tile([P, TOKEN_TILES, PAIRS], BF16)
        sin_sb = const.tile([P, TOKEN_TILES, PAIRS], BF16)
        nc.scalar.dma_start(out=cos_sb[:], in_=cos_rows)
        nc.scalar.dma_start(out=sin_sb[:], in_=sin_rows)
        x_raw = []

        def load_x(m):
            pieces = 2 if m == 0 else 1
            x_raw.append([])
            for c in range(pieces):
                raw = raw_pool.tile([P, D // pieces], BF16, name="x_raw%d_%d" % (m, c))
                nc.sync.dma_start(out=raw[:], in_=x_rows[m, :, c * D // pieces : (c + 1) * D // pieces])
                x_raw[m].append(raw[:])

        def load_unit(n):
            raw = raw_pool.tile([P, UNIT_TILES, D], BF16, name="w_raw%d" % n)
            if n < STRIDED_UNITS:
                for j in range(UNIT_TILES):
                    nc.sync.dma_start(out=raw[:, j, :], in_=w_units[n, :, j, :])
            else:
                nc.sync.dma_start(out=raw[:], in_=w_units[n, :, :, :])
            return raw

        load_x(0)
        load_x(1)
        w_raw = [load_unit(0)]
        load_x(2)
        load_x(3)
        w_raw += [load_unit(n) for n in range(1, LOADS_AHEAD)]

        idle = const.tile([P, BANK_COLS], BF16)
        nc.vector.memset(idle[:], 0.0)
        unused = flipped_pool.tile([P, BANK_PASSES, WORD_HALVES, P], F32, name="flipped")
        for i in range(WARM_UP_MATMULS):
            nc.tensor.matmul(
                out=unused[:].rearrange("p b u r -> p (b u r)"), lhsT=idle[:, 0:P], rhs=idle[:], start=True, stop=True
            )

        ident = const.tile([P, P], F32)
        make_identity(nc, ident[:])

        factors = const.tile([P, TOKEN_TILES, 2, UNIT_TILES, UNIT_HEADS, PAIRS], BF16)

        def make_factors():
            over_heads = [P, TOKEN_TILES, UNIT_HEADS, PAIRS]
            cos_heads = cos_sb[:].unsqueeze(2).to_broadcast(over_heads)
            sin_heads = sin_sb[:].unsqueeze(2).to_broadcast(over_heads)
            nc.vector.tensor_copy(out=factors[:, :, 0, 0, :, :], in_=cos_heads)
            nc.vector.tensor_copy(out=factors[:, :, 1, 0, :, :], in_=sin_heads)
            nc.vector.tensor_scalar_mul(out=factors[:, :, 0, 1, :, :], in0=sin_heads, scalar1=-1.0)
            nc.vector.tensor_copy(out=factors[:, :, 1, 1, :, :], in_=cos_heads)

        def put_in_order(copy, raw):
            ordered = ordered_pool.tile([P, D], BF16, name="ordered")
            copy(
                out=ordered[:].bitcast(F32).rearrange("p (g u m) -> p g u m", g=PASSES, u=WORD_HALVES),
                in_=raw.bitcast(F32).rearrange("p (g m u) -> p g u m", g=PASSES, u=WORD_HALVES),
            )
            return ordered

        def transpose_tile(pieces, is_ordered, target, copies):
            piece_words = WORDS // len(pieces)
            for first, copy in zip(range(0, PASSES, BANK_PASSES), copies):
                flipped = flipped_pool.tile([P, BANK_PASSES, WORD_HALVES, P], F32, name="flipped")
                for b in range(BANK_PASSES):
                    for u in range(WORD_HALVES):
                        place = (first + b) * WORD_HALVES * P
                        words = pieces[place // piece_words].bitcast(F32)
                        start = place % piece_words
                        if not is_ordered:
                            cols = words[:, start + u : start + WORD_HALVES * P : WORD_HALVES]
                        else:
                            cols = words[:, start + u * P : start + (u + 1) * P]
                        nc.tensor.transpose(flipped[:, b, u, :], cols, ident[:])
                copy(
                    out=target[:, first : first + BANK_PASSES, :, :], in_=flipped[:].rearrange("p b u r -> p b r u")
                )

        def quantise(grouped, rows, pool, name, calls=1):
            codes = pool.tile([P, PASSES, rows], U32, name=name + "_codes", align_bytes=64)
            scales = pool.tile([P, PASSES, rows], U8, name=name + "_scales", align_bytes=64)
            for c in range(calls):
                cols = slice(c * PASSES * rows // calls, (c + 1) * PASSES * rows // calls)
                nc.vector.quantize_mx(
                    out=codes[:].rearrange("p g c -> p (g c)")[:, cols].bitcast(FP8X4),
                    scales=scales[:].rearrange("p g c -> p (g c)")[:, cols],
                    in_=grouped[:, PACK * cols.start : PACK * cols.stop],
                )
            return codes, scales

        def multiply(token_tiles, w_unit):
            w_codes, w_scales = w_unit
            acc = acc_pool.tile([P, 2, UNIT], F32, name="acc")
            for j, m in enumerate(token_tiles):
                x_codes, x_scales = x_mx[m]
                for g in range(PASSES):
                    nc.tensor.matmul_mx(
                        out=acc[:, j, :],
                        lhsT=x_codes[:, g, :].bitcast(FP8X4),
                        lhsT_scale=x_scales[:, g, :],
                        rhs=w_codes[:, g, :].bitcast(FP8X4),
                        rhs_scale=w_scales[:, g, :],
                        start=(g == 0),
                        stop=(g == PASSES - 1),
                    )
            return acc

        def products(acc, tiles):
            shape = [P, 2, UNIT, 2]
            product = product_pool.tile(shape, F32, name="product")
            nc.vector.tensor_tensor(
                out=product[:],
                in0=acc[:].unsqueeze(3).to_broadcast(shape),
                in1=factors[:, tiles, :, :, :, :].rearrange("p m e j h i -> p m (j h i) e"),
                op=MULT,
            )
            return product

        def add_products(engine, product, rotated):
            engine.tensor_tensor(
                out=rotated,
                in0=product[:, :, 0:P, :].rearrange("p m r e -> p m (r e)"),
                in1=product[:, :, P:UNIT, :].rearrange("p m r e -> p m (r e)"),
                op=ADD,
            )

        def hold_gpsimd(scales):
            nc.gpsimd.tensor_copy(out=gate[:], in_=scales[:, 0, 0:4])

        def interleave(copy, sums, plain):
            copy(
                out=plain.rearrange("p (r j) -> p r j", j=UNIT_TILES),
                in_=sums.rearrange("p (j r) -> p r j", j=UNIT_TILES),
            )

        ordered = {(n, j): None for n in range(W_UNITS) for j in range(UNIT_TILES)}

        def order_tile(n, j, copy):
            ordered[n, j] = put_in_order(copy, w_raw[n][:, j, :])

        def order_unit(n):
            if n < W_UNITS:
                order_tile(n, 0, nc.scalar.copy)
                if n in SCALAR_ORDERS:
                    order_tile(n, 1, nc.scalar.copy)

        def new_grouped():
            return grouped_pool.tile([P, PASSES * UNIT * PACK], BF16, name="grouped", align_bytes=64)

        def transpose_tile_of_unit(n, j, grouped, copies):
            words = grouped[:].bitcast(F32).rearrange(
                "p (g j r u) -> p g j r u", g=PASSES, j=UNIT_TILES, u=WORD_HALVES
            )
            source = w_raw[n][:, j, :] if ordered[n, j] is None else ordered[n, j][:]
            transpose_tile([source], ordered[n, j] is not None, words[:, :, j, :, :], copies)

        gate = const.tile([P, 4], U8)
        make_factors()

        alone = [nc.scalar.copy, nc.scalar.copy]
        both = [nc.scalar.copy, nc.vector.tensor_copy]
        x_grouped = []
        x_mx = []

        def transpose_x(m):
            grouped = x_grouped_pool.tile([P, PASSES * P * PACK], BF16, name="x_grouped", align_bytes=64)
            words = grouped[:].bitcast(F32).rearrange("p (g r u) -> p g r u", g=PASSES, u=WORD_HALVES)
            transpose_tile(x_raw[m], False, words, alone)
            x_grouped.append(grouped)

        def quantise_x(m):
            x_mx.append(quantise(x_grouped[m], P, const, "x%d" % m))

        transpose_x(0)
        transpose_x(1)
        quantise_x(0)
        w_grouped = new_grouped()
        transpose_tile_of_unit(0, 0, w_grouped, both)
        quantise_x(1)
        transpose_tile_of_unit(0, 1, w_grouped, both)
        transpose_x(2)
        w_mx = quantise(w_grouped, UNIT, w_mx_pool, "w", calls=2)
        first_bank = multiply(range(2), w_mx)
        transpose_x(3)
        quantise_x(2)
        quantise_x(3)
        order_tile(STRIDED_UNITS, 0, nc.vector.tensor_copy)

        result = None
        late = None
        held = None
        for n in range(W_UNITS):
            if n + LOADS_AHEAD < W_UNITS:
                w_raw.append(load_unit(n + LOADS_AHEAD))
            following = n + 1 < W_UNITS
            if following:
                w_grouped = new_grouped()
                for j in range(UNIT_TILES):
                    transpose_tile_of_unit(n + 1, j, w_grouped, alone)
            order_unit(n + ORDER_AHEAD)
            step = 2 if following else 1
            starts = range(0 if n > 0 else step, TOKEN_TILES, step)
            banks = [multiply(range(m, m + step), w_mx) for m in starts]
            if n == 0:
                banks = [first_bank] + banks
            if following:
                w_mx = quantise(w_grouped, UNIT, w_mx_pool, "w")
            if held is not None:
                held()
                held = None
            if late is not None:
                if following:
                    hold_gpsimd(w_mx[1])
                late()
                late = None

            part = n % STORE_UNITS
            if part == 0 and n < ROTATED_UNITS:
                result = result_pool.tile([P, TOKEN_TILES, STORE_COLS], F32, name="result")

            def target(b, result=result, part=part):
                return result[:, 2 * b : 2 * b + 2, part * UNIT : (part + 1) * UNIT]

            def store(b, n=n, result=result, part=part):
                tiles = slice(2 * b, 2 * b + 2)
                stores = store_targets[n // STORE_UNITS]
                if n >= ROTATED_UNITS - STORE_UNITS:
                    cols = slice(part * UNIT, (part + 1) * UNIT)
                    nc.sync.dma_start(out=stores[:, tiles, cols], in_=result[:, tiles, cols])
                elif part == STORE_UNITS - 1:
                    nc.sync.dma_start(out=stores[:, tiles, :], in_=result[:, tiles, :])

            if n < ROTATED_UNITS:
                pair = [products(banks[b], slice(2 * b, 2 * b + 2)) for b in range(BANKS)]
                if n == ROTATED_UNITS - 1:
                    def held(pair=pair, target=target, store=store):
                        for b in range(BANKS):
                            add_products(nc.vector, pair[b], target(b))
                            store(b)

                else:
                    add_products(nc.vector, pair[0], target(0))
                    store(0)

                    def late(product=pair[1], target=target, store=store):
                        add_products(nc.gpsimd, product, target(1))
                        store(1)
            else:
                plain = plain_pool.tile([P, TOKEN_TILES, UNIT], F32, name="plain")
                helper = nc.scalar.copy if following else nc.vector.tensor_copy
                for m in range(TOKEN_TILES):
                    interleave(helper if m % 2 else nc.scalar.copy, banks[m // step][:, m % step, :], plain[:, m, :])
                    nc.sync.dma_start(out=v_rows[:, m, part * UNIT : (part + 1) * UNIT], in_=plain[:, m, :])
